import numpy as np
import ml_dtypes

BF16 = ml_dtypes.bfloat16


def bf(x):
    return np.asarray(x, np.float32).astype(BF16)


def f32(x):
    return np.asarray(x, np.float32)


def f64(x):
    return np.asarray(x).astype(np.float64)


def striped(idx):
    return np.tile(idx.reshape(-1, 16).T, (8, 1))


C, D, R, S, N, T, P = 512, 64, 32, 1024, 512, 256, 2
EPS = 1e-5


def rotate_half(v):
    w = v.reshape(C // D, D // R, R, N)
    return np.concatenate([-w[:, 1:], w[:, :1]], axis=1).reshape(C, N)


def setup_inputs():
    z = np.random.standard_normal((C, P, T))
    z = (z - z.mean(axis=(0, 1), keepdims=True)) / z.std(axis=(0, 1), keepdims=True) * np.sqrt(1.0 - EPS)
    ang = 2.0 * np.pi * np.random.random_sample((D, S))
    return {"x": f32(z.reshape(C, N)), "rope": f32(np.concatenate([np.cos(ang), np.sin(ang)], axis=0)), "offs": striped(np.random.permutation(np.tile(np.arange(S), 2))[:N])}


def reference(x, rope, offs):
    idx = offs[:16].T.reshape(-1)
    v = f64(x)
    cs = np.tile(f64(rope)[:D, idx], (C // D, 1))
    sn = np.tile(f64(rope)[D:, idx], (C // D, 1))
    return v * cs + rotate_half(v) * sn

@@ -1,0 +1,56 @@
+import concourse.mybir as mybir
+
+F32 = mybir.dt.float32
+U16 = mybir.dt.uint16
+MULT = mybir.AluOpType.mult
+ADD = mybir.AluOpType.add
+
+PARTITIONS = 128
+HEAD = 64
+HALF = 32
+
+
+def tile_model_lite_kernel(tc, x, rope, offs, out):
+    nc = tc.nc
+    channels, columns = x.shape
+    positions = rope.shape[1]
+    blocks = channels // PARTITIONS
+    heads_in_block = PARTITIONS // HEAD
+
+    with (
+        tc.tile_pool(name="held", bufs=1) as held,
+        tc.tile_pool(name="work", bufs=blocks) as work,
+    ):
+        offsets = held.tile([PARTITIONS, columns // 16], U16, name="offsets")
+        nc.sync.dma_start(offsets[:], offs)
+
+        cosines = held.tile([PARTITIONS, positions], F32, name="cosines")
+        sines = held.tile([PARTITIONS, positions], F32, name="sines")
+        for head in range(heads_in_block):
+            rows = slice(head * HEAD, (head + 1) * HEAD)
+            nc.sync.dma_start(cosines[rows, :], rope[0:HEAD, :])
+            nc.scalar.dma_start(sines[rows, :], rope[HEAD : 2 * HEAD, :])
+
+        for block in range(blocks):
+            first = block * PARTITIONS
+
+            straight = work.tile([PARTITIONS, columns], F32, name="straight")
+            nc.sync.dma_start(straight[:], x[first : first + PARTITIONS, :])
+
+            swapped = work.tile([PARTITIONS, columns], F32, name="swapped")
+            for head in range(heads_in_block):
+                low = head * HEAD
+                mid = low + HALF
+                high = low + HEAD
+                nc.scalar.dma_start(swapped[low:mid, :], x[first + mid : first + high, :])
+                nc.scalar.dma_start(swapped[mid:high, :], x[first + low : first + mid, :])
+                nc.scalar.mul(swapped[low:mid, :], swapped[low:mid, :], -1.0)
+
+            with_cosines = work.tile([PARTITIONS, columns], F32, name="with_cosines")
+            nc.vector.tensor_tensor(with_cosines[:], cosines[:].indirect(offsets[:]), straight[:], MULT)
+            with_sines = work.tile([PARTITIONS, columns], F32, name="with_sines")
+            nc.vector.tensor_tensor(with_sines[:], sines[:].indirect(offsets[:]), swapped[:], MULT)
+
+            rotated = work.tile([PARTITIONS, columns], F32, name="rotated")
+            nc.vector.tensor_tensor(rotated[:], with_cosines[:], with_sines[:], ADD)
+            nc.sync.dma_start(out[first : first + PARTITIONS, :], rotated[:])

@@ -1,13 +1,15 @@
 import concourse.mybir as mybir
+from concourse.masks import make_identity
 
 F32 = mybir.dt.float32
 U16 = mybir.dt.uint16
 MULT = mybir.AluOpType.mult
-ADD = mybir.AluOpType.add
 
 PARTITIONS = 128
 HEAD = 64
 HALF = 32
+
+FLOPS = 3 * 512 * 512
 
 
 def tile_model_lite_kernel(tc, x, rope, offs, out):
@@ -15,42 +17,44 @@ def tile_model_lite_kernel(tc, x, rope, offs, out):
     channels, columns = x.shape
     positions = rope.shape[1]
     blocks = channels // PARTITIONS
-    heads_in_block = PARTITIONS // HEAD
+    heads = [(low, low + HALF, low + HEAD) for low in range(0, PARTITIONS, HEAD)]
 
     with (
         tc.tile_pool(name="held", bufs=1) as held,
         tc.tile_pool(name="work", bufs=blocks) as work,
+        tc.psum_pool(name="sums", bufs=blocks) as sums,
     ):
         offsets = held.tile([PARTITIONS, columns // 16], U16, name="offsets")
         nc.sync.dma_start(offsets[:], offs)
 
         cosines = held.tile([PARTITIONS, positions], F32, name="cosines")
         sines = held.tile([PARTITIONS, positions], F32, name="sines")
-        for head in range(heads_in_block):
-            rows = slice(head * HEAD, (head + 1) * HEAD)
-            nc.sync.dma_start(cosines[rows, :], rope[0:HEAD, :])
-            nc.scalar.dma_start(sines[rows, :], rope[HEAD : 2 * HEAD, :])
+        for low, mid, high in heads:
+            nc.sync.dma_start(cosines[low:high, :], rope[0:HEAD, :])
+            nc.scalar.dma_start(sines[low:mid, :], rope[HEAD + HALF : 2 * HEAD, :])
+            nc.scalar.dma_start(sines[mid:high, :], rope[HEAD : HEAD + HALF, :])
+
+        keep = held.tile([PARTITIONS, PARTITIONS], F32, name="keep")
+        make_identity(nc, keep[:])
+        turn = held.tile([PARTITIONS, PARTITIONS], F32, name="turn")
+        for low, mid, high in heads:
+            nc.scalar.mul(turn[:, low:mid], keep[:, mid:high], -1.0)
+            nc.scalar.copy(turn[:, mid:high], keep[:, low:mid])
 
         for block in range(blocks):
             first = block * PARTITIONS
-
-            straight = work.tile([PARTITIONS, columns], F32, name="straight")
-            nc.sync.dma_start(straight[:], x[first : first + PARTITIONS, :])
-
-            swapped = work.tile([PARTITIONS, columns], F32, name="swapped")
-            for head in range(heads_in_block):
-                low = head * HEAD
-                mid = low + HALF
-                high = low + HEAD
-                nc.scalar.dma_start(swapped[low:mid, :], x[first + mid : first + high, :])
-                nc.scalar.dma_start(swapped[mid:high, :], x[first + low : first + mid, :])
-                nc.scalar.mul(swapped[low:mid, :], swapped[low:mid, :], -1.0)
+            rows = work.tile([PARTITIONS, columns], F32, name="rows")
+            nc.sync.dma_start(rows[:], x[first : first + PARTITIONS, :])
 
             with_cosines = work.tile([PARTITIONS, columns], F32, name="with_cosines")
-            nc.vector.tensor_tensor(with_cosines[:], cosines[:].indirect(offsets[:]), straight[:], MULT)
+            nc.vector.tensor_tensor(with_cosines[:], cosines[:].indirect(offsets[:]), rows[:], MULT)
             with_sines = work.tile([PARTITIONS, columns], F32, name="with_sines")
-            nc.vector.tensor_tensor(with_sines[:], sines[:].indirect(offsets[:]), swapped[:], MULT)
+            nc.vector.tensor_tensor(with_sines[:], sines[:].indirect(offsets[:]), rows[:], MULT)
+
+            total = sums.tile([PARTITIONS, columns], F32, name="total")
+            nc.tensor.matmul(total[:], keep[:], with_cosines[:], start=True, stop=False)
+            nc.tensor.matmul(total[:], turn[:], with_sines[:], start=False, stop=True)
 
             rotated = work.tile([PARTITIONS, columns], F32, name="rotated")
-            nc.vector.tensor_tensor(rotated[:], with_cosines[:], with_sines[:], ADD)
+            nc.scalar.copy(rotated[:], total[:])
             nc.sync.dma_start(out[first : first + PARTITIONS, :], rotated[:])

@@ -4,10 +4,13 @@ from concourse.masks import make_identity
 F32 = mybir.dt.float32
 U16 = mybir.dt.uint16
 MULT = mybir.AluOpType.mult
+ADD = mybir.AluOpType.add
 
 PARTITIONS = 128
 HEAD = 64
 HALF = 32
+
+LAST_PIECES = 2
 
 FLOPS = 3 * 512 * 512
 
@@ -18,6 +21,7 @@ def tile_model_lite_kernel(tc, x, rope, offs, out):
     positions = rope.shape[1]
     blocks = channels // PARTITIONS
     heads = [(low, low + HALF, low + HEAD) for low in range(0, PARTITIONS, HEAD)]
+    queues = (nc.sync, nc.scalar)
 
     with (
         tc.tile_pool(name="held", bufs=1) as held,
@@ -28,11 +32,22 @@ def tile_model_lite_kernel(tc, x, rope, offs, out):
         nc.sync.dma_start(offsets[:], offs)
 
         cosines = held.tile([PARTITIONS, positions], F32, name="cosines")
-        sines = held.tile([PARTITIONS, positions], F32, name="sines")
-        for low, mid, high in heads:
-            nc.sync.dma_start(cosines[low:high, :], rope[0:HEAD, :])
-            nc.scalar.dma_start(sines[low:mid, :], rope[HEAD + HALF : 2 * HEAD, :])
-            nc.scalar.dma_start(sines[mid:high, :], rope[HEAD : HEAD + HALF, :])
+        for queue, (low, mid, high) in zip(queues, heads):
+            queue.dma_start(cosines[low:high, :], rope[0:HEAD, :])
+
+        rows_of = []
+        for block in range(blocks):
+            first = block * PARTITIONS
+            rows = work.tile([PARTITIONS, columns], F32, name="rows")
+            for queue, (low, mid, high) in zip(queues, heads):
+                queue.dma_start(rows[low:high, :], x[first + low : first + high, :])
+            rows_of.append(rows)
+
+            if block == 0:
+                sines = held.tile([PARTITIONS, positions], F32, name="sines")
+                for queue, (low, mid, high) in zip(queues, heads):
+                    queue.dma_start(sines[low:mid, :], rope[HEAD + HALF : 2 * HEAD, :])
+                    queue.dma_start(sines[mid:high, :], rope[HEAD : HEAD + HALF, :])
 
         keep = held.tile([PARTITIONS, PARTITIONS], F32, name="keep")
         make_identity(nc, keep[:])
@@ -43,18 +58,27 @@ def tile_model_lite_kernel(tc, x, rope, offs, out):
 
         for block in range(blocks):
             first = block * PARTITIONS
-            rows = work.tile([PARTITIONS, columns], F32, name="rows")
-            nc.sync.dma_start(rows[:], x[first : first + PARTITIONS, :])
+            rows = rows_of[block]
 
             with_cosines = work.tile([PARTITIONS, columns], F32, name="with_cosines")
             nc.vector.tensor_tensor(with_cosines[:], cosines[:].indirect(offsets[:]), rows[:], MULT)
             with_sines = work.tile([PARTITIONS, columns], F32, name="with_sines")
-            nc.vector.tensor_tensor(with_sines[:], sines[:].indirect(offsets[:]), rows[:], MULT)
-
-            total = sums.tile([PARTITIONS, columns], F32, name="total")
-            nc.tensor.matmul(total[:], keep[:], with_cosines[:], start=True, stop=False)
-            nc.tensor.matmul(total[:], turn[:], with_sines[:], start=False, stop=True)
-
             rotated = work.tile([PARTITIONS, columns], F32, name="rotated")
-            nc.scalar.copy(rotated[:], total[:])
-            nc.sync.dma_start(out[first : first + PARTITIONS, :], rotated[:])
+
+            if block < blocks - 1:
+                nc.vector.tensor_tensor(with_sines[:], sines[:].indirect(offsets[:]), rows[:], MULT)
+                total = sums.tile([PARTITIONS, columns], F32, name="total")
+                nc.tensor.matmul(total[:], keep[:], with_cosines[:], start=True, stop=False)
+                nc.tensor.matmul(total[:], turn[:], with_sines[:], start=False, stop=True)
+                nc.scalar.copy(rotated[:], total[:])
+                nc.sync.dma_start(out[first : first + PARTITIONS, :], rotated[:])
+            else:
+                width = columns // LAST_PIECES
+                for piece in range(LAST_PIECES):
+                    cols = slice(piece * width, (piece + 1) * width)
+                    entries = offsets[:, piece * (width // 16) : (piece + 1) * (width // 16)]
+                    nc.vector.tensor_tensor(with_sines[:, cols], sines[:].indirect(entries), rows[:, cols], MULT)
+                    turned = sums.tile([PARTITIONS, width], F32, name="turned")
+                    nc.tensor.matmul(turned[:], turn[:], with_sines[:, cols], start=True, stop=True)
+                    nc.vector.tensor_tensor(rotated[:, cols], with_cosines[:, cols], turned[:], ADD)
+                    nc.sync.dma_start(out[first : first + PARTITIONS, cols], rotated[:, cols])

@@ -4,13 +4,10 @@ from concourse.masks import make_identity
 F32 = mybir.dt.float32
 U16 = mybir.dt.uint16
 MULT = mybir.AluOpType.mult
-ADD = mybir.AluOpType.add
 
 PARTITIONS = 128
 HEAD = 64
 HALF = 32
-
-LAST_PIECES = 2
 
 FLOPS = 3 * 512 * 512
 
@@ -63,22 +60,12 @@ def tile_model_lite_kernel(tc, x, rope, offs, out):
             with_cosines = work.tile([PARTITIONS, columns], F32, name="with_cosines")
             nc.vector.tensor_tensor(with_cosines[:], cosines[:].indirect(offsets[:]), rows[:], MULT)
             with_sines = work.tile([PARTITIONS, columns], F32, name="with_sines")
-            rotated = work.tile([PARTITIONS, columns], F32, name="rotated")
+            nc.vector.tensor_tensor(with_sines[:], sines[:].indirect(offsets[:]), rows[:], MULT)
 
-            if block < blocks - 1:
-                nc.vector.tensor_tensor(with_sines[:], sines[:].indirect(offsets[:]), rows[:], MULT)
-                total = sums.tile([PARTITIONS, columns], F32, name="total")
-                nc.tensor.matmul(total[:], keep[:], with_cosines[:], start=True, stop=False)
-                nc.tensor.matmul(total[:], turn[:], with_sines[:], start=False, stop=True)
-                nc.scalar.copy(rotated[:], total[:])
-                nc.sync.dma_start(out[first : first + PARTITIONS, :], rotated[:])
-            else:
-                width = columns // LAST_PIECES
-                for piece in range(LAST_PIECES):
-                    cols = slice(piece * width, (piece + 1) * width)
-                    entries = offsets[:, piece * (width // 16) : (piece + 1) * (width // 16)]
-                    nc.vector.tensor_tensor(with_sines[:, cols], sines[:].indirect(entries), rows[:, cols], MULT)
-                    turned = sums.tile([PARTITIONS, width], F32, name="turned")
-                    nc.tensor.matmul(turned[:], turn[:], with_sines[:, cols], start=True, stop=True)
-                    nc.vector.tensor_tensor(rotated[:, cols], with_cosines[:, cols], turned[:], ADD)
-                    nc.sync.dma_start(out[first : first + PARTITIONS, cols], rotated[:, cols])
+            total = sums.tile([PARTITIONS, columns], F32, name="total")
+            nc.tensor.matmul(total[:], keep[:], with_cosines[:], start=True, stop=False)
+            nc.tensor.matmul(total[:], turn[:], with_sines[:], start=False, stop=True)
+
+            rotated = work.tile([PARTITIONS, columns], F32, name="rotated")
+            nc.scalar.copy(rotated[:], total[:])
+            nc.sync.dma_start(out[first : first + PARTITIONS, :], rotated[:])

@@ -4,10 +4,13 @@ from concourse.masks import make_identity
 F32 = mybir.dt.float32
 U16 = mybir.dt.uint16
 MULT = mybir.AluOpType.mult
+ADD = mybir.AluOpType.add
 
 PARTITIONS = 128
 HEAD = 64
 HALF = 32
+
+LAST_PIECES = 2
 
 FLOPS = 3 * 512 * 512
 
@@ -18,7 +21,6 @@ def tile_model_lite_kernel(tc, x, rope, offs, out):
     positions = rope.shape[1]
     blocks = channels // PARTITIONS
     heads = [(low, low + HALF, low + HEAD) for low in range(0, PARTITIONS, HEAD)]
-    queues = (nc.sync, nc.scalar)
 
     with (
         tc.tile_pool(name="held", bufs=1) as held,
@@ -29,22 +31,21 @@ def tile_model_lite_kernel(tc, x, rope, offs, out):
         nc.sync.dma_start(offsets[:], offs)
 
         cosines = held.tile([PARTITIONS, positions], F32, name="cosines")
-        for queue, (low, mid, high) in zip(queues, heads):
-            queue.dma_start(cosines[low:high, :], rope[0:HEAD, :])
+        for low, mid, high in heads:
+            nc.sync.dma_start(cosines[low:high, :], rope[0:HEAD, :])
 
         rows_of = []
         for block in range(blocks):
             first = block * PARTITIONS
             rows = work.tile([PARTITIONS, columns], F32, name="rows")
-            for queue, (low, mid, high) in zip(queues, heads):
-                queue.dma_start(rows[low:high, :], x[first + low : first + high, :])
+            nc.sync.dma_start(rows[:], x[first : first + PARTITIONS, :])
             rows_of.append(rows)
 
             if block == 0:
                 sines = held.tile([PARTITIONS, positions], F32, name="sines")
-                for queue, (low, mid, high) in zip(queues, heads):
-                    queue.dma_start(sines[low:mid, :], rope[HEAD + HALF : 2 * HEAD, :])
-                    queue.dma_start(sines[mid:high, :], rope[HEAD : HEAD + HALF, :])
+                for low, mid, high in heads:
+                    nc.sync.dma_start(sines[low:mid, :], rope[HEAD + HALF : 2 * HEAD, :])
+                    nc.sync.dma_start(sines[mid:high, :], rope[HEAD : HEAD + HALF, :])
 
         keep = held.tile([PARTITIONS, PARTITIONS], F32, name="keep")
         make_identity(nc, keep[:])
@@ -60,12 +61,22 @@ def tile_model_lite_kernel(tc, x, rope, offs, out):
             with_cosines = work.tile([PARTITIONS, columns], F32, name="with_cosines")
             nc.vector.tensor_tensor(with_cosines[:], cosines[:].indirect(offsets[:]), rows[:], MULT)
             with_sines = work.tile([PARTITIONS, columns], F32, name="with_sines")
-            nc.vector.tensor_tensor(with_sines[:], sines[:].indirect(offsets[:]), rows[:], MULT)
-
-            total = sums.tile([PARTITIONS, columns], F32, name="total")
-            nc.tensor.matmul(total[:], keep[:], with_cosines[:], start=True, stop=False)
-            nc.tensor.matmul(total[:], turn[:], with_sines[:], start=False, stop=True)
-
             rotated = work.tile([PARTITIONS, columns], F32, name="rotated")
-            nc.scalar.copy(rotated[:], total[:])
-            nc.sync.dma_start(out[first : first + PARTITIONS, :], rotated[:])
+
+            if block < blocks - 1:
+                nc.vector.tensor_tensor(with_sines[:], sines[:].indirect(offsets[:]), rows[:], MULT)
+                total = sums.tile([PARTITIONS, columns], F32, name="total")
+                nc.tensor.matmul(total[:], keep[:], with_cosines[:], start=True, stop=False)
+                nc.tensor.matmul(total[:], turn[:], with_sines[:], start=False, stop=True)
+                nc.scalar.copy(rotated[:], total[:])
+                nc.sync.dma_start(out[first : first + PARTITIONS, :], rotated[:])
+            else:
+                width = columns // LAST_PIECES
+                for piece in range(LAST_PIECES):
+                    cols = slice(piece * width, (piece + 1) * width)
+                    entries = offsets[:, piece * (width // 16) : (piece + 1) * (width // 16)]
+                    nc.vector.tensor_tensor(with_sines[:, cols], sines[:].indirect(entries), rows[:, cols], MULT)
+                    turned = sums.tile([PARTITIONS, width], F32, name="turned")
+                    nc.tensor.matmul(turned[:], turn[:], with_sines[:, cols], start=True, stop=True)
+                    nc.vector.tensor_tensor(rotated[:, cols], with_cosines[:, cols], turned[:], ADD)
+                    nc.sync.dma_start(out[first : first + PARTITIONS, cols], rotated[:, cols])

@@ -9,8 +9,7 @@ ADD = mybir.AluOpType.add
 PARTITIONS = 128
 HEAD = 64
 HALF = 32
-
-LAST_PIECES = 2
+PIECES = 2
 
 FLOPS = 3 * 512 * 512
 
@@ -20,6 +19,8 @@ def tile_model_lite_kernel(tc, x, rope, offs, out):
     channels, columns = x.shape
     positions = rope.shape[1]
     blocks = channels // PARTITIONS
+    early = range(0, blocks // 2)
+    late = range(blocks // 2, blocks)
     heads = [(low, low + HALF, low + HEAD) for low in range(0, PARTITIONS, HEAD)]
 
     with (
@@ -34,18 +35,17 @@ def tile_model_lite_kernel(tc, x, rope, offs, out):
         for low, mid, high in heads:
             nc.sync.dma_start(cosines[low:high, :], rope[0:HEAD, :])
 
-        rows_of = []
-        for block in range(blocks):
-            first = block * PARTITIONS
-            rows = work.tile([PARTITIONS, columns], F32, name="rows")
-            nc.sync.dma_start(rows[:], x[first : first + PARTITIONS, :])
-            rows_of.append(rows)
+        rows_of = [work.tile([PARTITIONS, columns], F32, name="rows") for block in range(blocks)]
+        for block in early:
+            nc.sync.dma_start(rows_of[block][:], x[block * PARTITIONS : (block + 1) * PARTITIONS, :])
 
-            if block == 0:
-                sines = held.tile([PARTITIONS, positions], F32, name="sines")
-                for low, mid, high in heads:
-                    nc.sync.dma_start(sines[low:mid, :], rope[HEAD + HALF : 2 * HEAD, :])
-                    nc.sync.dma_start(sines[mid:high, :], rope[HEAD : HEAD + HALF, :])
+        sines = held.tile([PARTITIONS, positions], F32, name="sines")
+        for low, mid, high in heads:
+            nc.sync.dma_start(sines[low:mid, :], rope[HEAD + HALF : 2 * HEAD, :])
+            nc.sync.dma_start(sines[mid:high, :], rope[HEAD : HEAD + HALF, :])
+
+        for block in late:
+            nc.sync.dma_start(rows_of[block][:], x[block * PARTITIONS : (block + 1) * PARTITIONS, :])
 
         keep = held.tile([PARTITIONS, PARTITIONS], F32, name="keep")
         make_identity(nc, keep[:])
@@ -54,29 +54,28 @@ def tile_model_lite_kernel(tc, x, rope, offs, out):
             nc.scalar.mul(turn[:, low:mid], keep[:, mid:high], -1.0)
             nc.scalar.copy(turn[:, mid:high], keep[:, low:mid])
 
-        for block in range(blocks):
-            first = block * PARTITIONS
-            rows = rows_of[block]
+        total_of = [sums.tile([PARTITIONS, columns], F32, name="total") for block in range(blocks)]
 
+        for block in early:
             with_cosines = work.tile([PARTITIONS, columns], F32, name="with_cosines")
-            nc.vector.tensor_tensor(with_cosines[:], cosines[:].indirect(offsets[:]), rows[:], MULT)
-            with_sines = work.tile([PARTITIONS, columns], F32, name="with_sines")
-            rotated = work.tile([PARTITIONS, columns], F32, name="rotated")
+            nc.vector.tensor_tensor(with_cosines[:], cosines[:].indirect(offsets[:]), rows_of[block][:], MULT)
+            nc.tensor.matmul(total_of[block][:], keep[:], with_cosines[:], start=True, stop=False)
 
-            if block < blocks - 1:
-                nc.vector.tensor_tensor(with_sines[:], sines[:].indirect(offsets[:]), rows[:], MULT)
-                total = sums.tile([PARTITIONS, columns], F32, name="total")
-                nc.tensor.matmul(total[:], keep[:], with_cosines[:], start=True, stop=False)
-                nc.tensor.matmul(total[:], turn[:], with_sines[:], start=False, stop=True)
-                nc.scalar.copy(rotated[:], total[:])
-                nc.sync.dma_start(out[first : first + PARTITIONS, :], rotated[:])
-            else:
-                width = columns // LAST_PIECES
-                for piece in range(LAST_PIECES):
-                    cols = slice(piece * width, (piece + 1) * width)
-                    entries = offsets[:, piece * (width // 16) : (piece + 1) * (width // 16)]
-                    nc.vector.tensor_tensor(with_sines[:, cols], sines[:].indirect(entries), rows[:, cols], MULT)
-                    turned = sums.tile([PARTITIONS, width], F32, name="turned")
-                    nc.tensor.matmul(turned[:], turn[:], with_sines[:, cols], start=True, stop=True)
-                    nc.vector.tensor_tensor(rotated[:, cols], with_cosines[:, cols], turned[:], ADD)
-                    nc.sync.dma_start(out[first : first + PARTITIONS, cols], rotated[:, cols])
+        for block in range(blocks):
+            with_sines = work.tile([PARTITIONS, columns], F32, name="with_sines")
+            nc.vector.tensor_tensor(with_sines[:], sines[:].indirect(offsets[:]), rows_of[block][:], MULT)
+            nc.tensor.matmul(total_of[block][:], turn[:], with_sines[:], start=(block in late), stop=True)
+            if block in early:
+                rotated = work.tile([PARTITIONS, columns], F32, name="rotated")
+                nc.scalar.copy(rotated[:], total_of[block][:])
+                nc.sync.dma_start(out[block * PARTITIONS : (block + 1) * PARTITIONS, :], rotated[:])
+
+        width = columns // PIECES
+        for block in late:
+            with_cosines = work.tile([PARTITIONS, columns], F32, name="with_cosines")
+            nc.vector.tensor_tensor(with_cosines[:], cosines[:].indirect(offsets[:]), rows_of[block][:], MULT)
+            rotated = work.tile([PARTITIONS, columns], F32, name="rotated")
+            for piece in range(PIECES):
+                cols = slice(piece * width, (piece + 1) * width)
+                nc.vector.tensor_tensor(rotated[:, cols], with_cosines[:, cols], total_of[block][:, cols], ADD)
+                nc.sync.dma_start(out[block * PARTITIONS : (block + 1) * PARTITIONS, cols], rotated[:, cols])

@@ -10,6 +10,7 @@ PARTITIONS = 128
 HEAD = 64
 HALF = 32
 PIECES = 2
+WARM_UP = 12
 
 FLOPS = 3 * 512 * 512
 
@@ -27,6 +28,7 @@ def tile_model_lite_kernel(tc, x, rope, offs, out):
         tc.tile_pool(name="held", bufs=1) as held,
         tc.tile_pool(name="work", bufs=blocks) as work,
         tc.psum_pool(name="sums", bufs=blocks) as sums,
+        tc.psum_pool(name="scratch", bufs=1) as scratch,
     ):
         offsets = held.tile([PARTITIONS, columns // 16], U16, name="offsets")
         nc.sync.dma_start(offsets[:], offs)
@@ -53,6 +55,10 @@ def tile_model_lite_kernel(tc, x, rope, offs, out):
         for low, mid, high in heads:
             nc.scalar.mul(turn[:, low:mid], keep[:, mid:high], -1.0)
             nc.scalar.copy(turn[:, mid:high], keep[:, low:mid])
+
+        warm = scratch.tile([PARTITIONS, PARTITIONS], F32, name="warm")
+        for repeat in range(WARM_UP):
+            nc.tensor.matmul(warm[:], keep[:], keep[:], start=True, stop=True)
 
         total_of = [sums.tile([PARTITIONS, columns], F32, name="total") for block in range(blocks)]
 

@@ -9,6 +9,7 @@ ADD = mybir.AluOpType.add
 PARTITIONS = 128
 HEAD = 64
 HALF = 32
+PAIR = PARTITIONS // HEAD
 PIECES = 2
 WARM_UP = 12
 
@@ -22,7 +23,12 @@ def tile_model_lite_kernel(tc, x, rope, offs, out):
     blocks = channels // PARTITIONS
     early = range(0, blocks // 2)
     late = range(blocks // 2, blocks)
-    heads = [(low, low + HALF, low + HEAD) for low in range(0, PARTITIONS, HEAD)]
+
+    def by_head(tile):
+        return tile.rearrange("(f a) c -> a f c", a=PAIR)
+
+    def head_rows(block, a):
+        return slice((block * PAIR + a) * HEAD, (block * PAIR + a + 1) * HEAD)
 
     with (
         tc.tile_pool(name="held", bufs=1) as held,
@@ -34,27 +40,29 @@ def tile_model_lite_kernel(tc, x, rope, offs, out):
         nc.sync.dma_start(offsets[:], offs)
 
         cosines = held.tile([PARTITIONS, positions], F32, name="cosines")
-        for low, mid, high in heads:
-            nc.sync.dma_start(cosines[low:high, :], rope[0:HEAD, :])
+        for a in range(PAIR):
+            nc.sync.dma_start(by_head(cosines[:])[a], rope[0:HEAD, :])
 
         rows_of = [work.tile([PARTITIONS, columns], F32, name="rows") for block in range(blocks)]
         for block in early:
-            nc.sync.dma_start(rows_of[block][:], x[block * PARTITIONS : (block + 1) * PARTITIONS, :])
+            for a in range(PAIR):
+                nc.sync.dma_start(by_head(rows_of[block][:])[a], x[head_rows(block, a), :])
 
         sines = held.tile([PARTITIONS, positions], F32, name="sines")
-        for low, mid, high in heads:
-            nc.sync.dma_start(sines[low:mid, :], rope[HEAD + HALF : 2 * HEAD, :])
-            nc.sync.dma_start(sines[mid:high, :], rope[HEAD : HEAD + HALF, :])
+        for a in range(PAIR):
+            nc.sync.dma_start(by_head(sines[:])[a, 0:HALF], rope[HEAD + HALF : 2 * HEAD, :])
+            nc.sync.dma_start(by_head(sines[:])[a, HALF:HEAD], rope[HEAD : HEAD + HALF, :])
 
         for block in late:
-            nc.sync.dma_start(rows_of[block][:], x[block * PARTITIONS : (block + 1) * PARTITIONS, :])
+            for a in range(PAIR):
+                nc.sync.dma_start(by_head(rows_of[block][:])[a], x[head_rows(block, a), :])
 
         keep = held.tile([PARTITIONS, PARTITIONS], F32, name="keep")
         make_identity(nc, keep[:])
         turn = held.tile([PARTITIONS, PARTITIONS], F32, name="turn")
-        for low, mid, high in heads:
-            nc.scalar.mul(turn[:, low:mid], keep[:, mid:high], -1.0)
-            nc.scalar.copy(turn[:, mid:high], keep[:, low:mid])
+        middle = PARTITIONS // 2
+        nc.scalar.mul(turn[:, 0:middle], keep[:, middle:PARTITIONS], -1.0)
+        nc.scalar.copy(turn[:, middle:PARTITIONS], keep[:, 0:middle])
 
         warm = scratch.tile([PARTITIONS, PARTITIONS], F32, name="warm")
         for repeat in range(WARM_UP):
@@ -74,7 +82,8 @@ def tile_model_lite_kernel(tc, x, rope, offs, out):
             if block in early:
                 rotated = work.tile([PARTITIONS, columns], F32, name="rotated")
                 nc.scalar.copy(rotated[:], total_of[block][:])
-                nc.sync.dma_start(out[block * PARTITIONS : (block + 1) * PARTITIONS, :], rotated[:])
+                for a in range(PAIR):
+                    nc.sync.dma_start(out[head_rows(block, a), :], by_head(rotated[:])[a])
 
         width = columns // PIECES
         for block in late:
@@ -84,4 +93,5 @@ def tile_model_lite_kernel(tc, x, rope, offs, out):
             for piece in range(PIECES):
                 cols = slice(piece * width, (piece + 1) * width)
                 nc.vector.tensor_tensor(rotated[:, cols], with_cosines[:, cols], total_of[block][:, cols], ADD)
-                nc.sync.dma_start(out[block * PARTITIONS : (block + 1) * PARTITIONS, cols], rotated[:, cols])
+                for a in range(PAIR):
+                    nc.sync.dma_start(out[head_rows(block, a), cols], by_head(rotated[:, cols])[a])

@@ -11,7 +11,8 @@ HEAD = 64
 HALF = 32
 PAIR = PARTITIONS // HEAD
 PIECES = 2
-WARM_UP = 12
+LEAD = 128
+WARM_UP = 8
 
 FLOPS = 3 * 512 * 512
 
@@ -21,8 +22,7 @@ def tile_model_lite_kernel(tc, x, rope, offs, out):
     channels, columns = x.shape
     positions = rope.shape[1]
     blocks = channels // PARTITIONS
-    early = range(0, blocks // 2)
-    late = range(blocks // 2, blocks)
+    last = blocks - 1
 
     def by_head(tile):
         return tile.rearrange("(f a) c -> a f c", a=PAIR)
@@ -33,7 +33,7 @@ def tile_model_lite_kernel(tc, x, rope, offs, out):
     with (
         tc.tile_pool(name="held", bufs=1) as held,
         tc.tile_pool(name="work", bufs=blocks) as work,
-        tc.psum_pool(name="sums", bufs=blocks) as sums,
+        tc.psum_pool(name="sums", bufs=last) as sums,
         tc.psum_pool(name="scratch", bufs=1) as scratch,
     ):
         offsets = held.tile([PARTITIONS, columns // 16], U16, name="offsets")
@@ -44,18 +44,22 @@ def tile_model_lite_kernel(tc, x, rope, offs, out):
             nc.sync.dma_start(by_head(cosines[:])[a], rope[0:HEAD, :])
 
         rows_of = [work.tile([PARTITIONS, columns], F32, name="rows") for block in range(blocks)]
-        for block in early:
+
+        def load_rows(block, begin, end):
             for a in range(PAIR):
-                nc.sync.dma_start(by_head(rows_of[block][:])[a], x[head_rows(block, a), :])
+                nc.sync.dma_start(by_head(rows_of[block][:, begin:end])[a], x[head_rows(block, a), begin:end])
+
+        load_rows(0, 0, LEAD)
+        load_rows(0, LEAD, columns)
+        for block in range(1, last):
+            load_rows(block, 0, columns)
 
         sines = held.tile([PARTITIONS, positions], F32, name="sines")
         for a in range(PAIR):
             nc.sync.dma_start(by_head(sines[:])[a, 0:HALF], rope[HEAD + HALF : 2 * HEAD, :])
             nc.sync.dma_start(by_head(sines[:])[a, HALF:HEAD], rope[HEAD : HEAD + HALF, :])
 
-        for block in late:
-            for a in range(PAIR):
-                nc.sync.dma_start(by_head(rows_of[block][:])[a], x[head_rows(block, a), :])
+        load_rows(last, 0, columns)
 
         keep = held.tile([PARTITIONS, PARTITIONS], F32, name="keep")
         make_identity(nc, keep[:])
@@ -68,30 +72,39 @@ def tile_model_lite_kernel(tc, x, rope, offs, out):
         for repeat in range(WARM_UP):
             nc.tensor.matmul(warm[:], keep[:], keep[:], start=True, stop=True)
 
-        total_of = [sums.tile([PARTITIONS, columns], F32, name="total") for block in range(blocks)]
+        total_of = [sums.tile([PARTITIONS, columns], F32, name="total") for block in range(last)]
 
-        for block in early:
+        for block in range(last):
             with_cosines = work.tile([PARTITIONS, columns], F32, name="with_cosines")
-            nc.vector.tensor_tensor(with_cosines[:], cosines[:].indirect(offsets[:]), rows_of[block][:], MULT)
+            for begin, end in [(0, LEAD), (LEAD, columns)] if block == 0 else [(0, columns)]:
+                nc.vector.tensor_tensor(
+                    with_cosines[:, begin:end],
+                    cosines[:].indirect(offsets[:, begin // 16 : end // 16]),
+                    rows_of[block][:, begin:end],
+                    MULT,
+                )
             nc.tensor.matmul(total_of[block][:], keep[:], with_cosines[:], start=True, stop=False)
 
-        for block in range(blocks):
+        for block in range(last):
             with_sines = work.tile([PARTITIONS, columns], F32, name="with_sines")
             nc.vector.tensor_tensor(with_sines[:], sines[:].indirect(offsets[:]), rows_of[block][:], MULT)
-            nc.tensor.matmul(total_of[block][:], turn[:], with_sines[:], start=(block in late), stop=True)
-            if block in early:
-                rotated = work.tile([PARTITIONS, columns], F32, name="rotated")
-                nc.scalar.copy(rotated[:], total_of[block][:])
-                for a in range(PAIR):
-                    nc.sync.dma_start(out[head_rows(block, a), :], by_head(rotated[:])[a])
+            nc.tensor.matmul(total_of[block][:], turn[:], with_sines[:], start=False, stop=True)
+            rotated = work.tile([PARTITIONS, columns], F32, name="rotated")
+            nc.scalar.copy(rotated[:], total_of[block][:])
+            for a in range(PAIR):
+                nc.sync.dma_start(out[head_rows(block, a), :], by_head(rotated[:])[a])
 
         width = columns // PIECES
-        for block in late:
-            with_cosines = work.tile([PARTITIONS, columns], F32, name="with_cosines")
-            nc.vector.tensor_tensor(with_cosines[:], cosines[:].indirect(offsets[:]), rows_of[block][:], MULT)
-            rotated = work.tile([PARTITIONS, columns], F32, name="rotated")
-            for piece in range(PIECES):
-                cols = slice(piece * width, (piece + 1) * width)
-                nc.vector.tensor_tensor(rotated[:, cols], with_cosines[:, cols], total_of[block][:, cols], ADD)
-                for a in range(PAIR):
-                    nc.sync.dma_start(out[head_rows(block, a), cols], by_head(rotated[:, cols])[a])
+        pieces = [slice(piece * width, (piece + 1) * width) for piece in range(PIECES)]
+        with_sines = work.tile([PARTITIONS, columns], F32, name="with_sines")
+        nc.vector.tensor_tensor(with_sines[:], sines[:].indirect(offsets[:]), rows_of[last][:], MULT)
+        turned_of = [sums.tile([PARTITIONS, width], F32, name="turned") for cols in pieces]
+        for cols, turned in zip(pieces, turned_of):
+            nc.tensor.matmul(turned[:], turn[:], with_sines[:, cols], start=True, stop=True)
+        with_cosines = work.tile([PARTITIONS, columns], F32, name="with_cosines")
+        nc.vector.tensor_tensor(with_cosines[:], cosines[:].indirect(offsets[:]), rows_of[last][:], MULT)
+        rotated = work.tile([PARTITIONS, columns], F32, name="rotated")
+        for cols, turned in zip(pieces, turned_of):
+            nc.vector.tensor_tensor(rotated[:, cols], with_cosines[:, cols], turned[:], ADD)
+            for a in range(PAIR):
+                nc.sync.dma_start(out[head_rows(last, a), cols], by_head(rotated[:, cols])[a])

@@ -12,7 +12,6 @@ HALF = 32
 PAIR = PARTITIONS // HEAD
 PIECES = 2
 LEAD = 128
-WARM_UP = 8
 
 FLOPS = 3 * 512 * 512
 
@@ -33,8 +32,7 @@ def tile_model_lite_kernel(tc, x, rope, offs, out):
     with (
         tc.tile_pool(name="held", bufs=1) as held,
         tc.tile_pool(name="work", bufs=blocks) as work,
-        tc.psum_pool(name="sums", bufs=last) as sums,
-        tc.psum_pool(name="scratch", bufs=1) as scratch,
+        tc.psum_pool(name="sums", bufs=last + 1 + PIECES) as sums,
     ):
         offsets = held.tile([PARTITIONS, columns // 16], U16, name="offsets")
         nc.sync.dma_start(offsets[:], offs)
@@ -49,10 +47,10 @@ def tile_model_lite_kernel(tc, x, rope, offs, out):
             for a in range(PAIR):
                 nc.sync.dma_start(by_head(rows_of[block][:, begin:end])[a], x[head_rows(block, a), begin:end])
 
-        load_rows(0, 0, LEAD)
-        load_rows(0, LEAD, columns)
-        for block in range(1, last):
-            load_rows(block, 0, columns)
+        parts_of = [[(0, LEAD), (LEAD, columns)]] + [[(0, columns)] for block in range(1, last)]
+        for block in range(last):
+            for begin, end in parts_of[block]:
+                load_rows(block, begin, end)
 
         sines = held.tile([PARTITIONS, positions], F32, name="sines")
         for a in range(PAIR):
@@ -68,29 +66,25 @@ def tile_model_lite_kernel(tc, x, rope, offs, out):
         nc.scalar.mul(turn[:, 0:middle], keep[:, middle:PARTITIONS], -1.0)
         nc.scalar.copy(turn[:, middle:PARTITIONS], keep[:, 0:middle])
 
-        warm = scratch.tile([PARTITIONS, PARTITIONS], F32, name="warm")
-        for repeat in range(WARM_UP):
-            nc.tensor.matmul(warm[:], keep[:], keep[:], start=True, stop=True)
-
-        total_of = [sums.tile([PARTITIONS, columns], F32, name="total") for block in range(last)]
-
+        total_of = [[sums.tile([PARTITIONS, end - begin], F32, name="total") for begin, end in parts] for parts in parts_of]
         for block in range(last):
             with_cosines = work.tile([PARTITIONS, columns], F32, name="with_cosines")
-            for begin, end in [(0, LEAD), (LEAD, columns)] if block == 0 else [(0, columns)]:
+            for (begin, end), total in zip(parts_of[block], total_of[block]):
                 nc.vector.tensor_tensor(
                     with_cosines[:, begin:end],
                     cosines[:].indirect(offsets[:, begin // 16 : end // 16]),
                     rows_of[block][:, begin:end],
                     MULT,
                 )
-            nc.tensor.matmul(total_of[block][:], keep[:], with_cosines[:], start=True, stop=False)
+                nc.tensor.matmul(total[:], keep[:], with_cosines[:, begin:end], start=True, stop=False)
 
         for block in range(last):
             with_sines = work.tile([PARTITIONS, columns], F32, name="with_sines")
             nc.vector.tensor_tensor(with_sines[:], sines[:].indirect(offsets[:]), rows_of[block][:], MULT)
-            nc.tensor.matmul(total_of[block][:], turn[:], with_sines[:], start=False, stop=True)
             rotated = work.tile([PARTITIONS, columns], F32, name="rotated")
-            nc.scalar.copy(rotated[:], total_of[block][:])
+            for (begin, end), total in zip(parts_of[block], total_of[block]):
+                nc.tensor.matmul(total[:], turn[:], with_sines[:, begin:end], start=False, stop=True)
+                nc.scalar.copy(rotated[:, begin:end], total[:])
             for a in range(PAIR):
                 nc.sync.dma_start(out[head_rows(block, a), :], by_head(rotated[:])[a])
 
@@ -98,7 +92,7 @@ def tile_model_lite_kernel(tc, x, rope, offs, out):
         pieces = [slice(piece * width, (piece + 1) * width) for piece in range(PIECES)]
         with_sines = work.tile([PARTITIONS, columns], F32, name="with_sines")
         nc.vector.tensor_tensor(with_sines[:], sines[:].indirect(offsets[:]), rows_of[last][:], MULT)
-        turned_of = [sums.tile([PARTITIONS, width], F32, name="turned") for cols in pieces]
+        turned_of = [sums.tile([PARTITIONS, width], F32, name="total") for cols in pieces]
         for cols, turned in zip(pieces, turned_of):
             nc.tensor.matmul(turned[:], turn[:], with_sines[:, cols], start=True, stop=True)
         with_cosines = work.tile([PARTITIONS, columns], F32, name="with_cosines")

@@ -26,6 +26,8 @@ def tile_model_lite_kernel(tc, x, rope, offs, out):
     def by_head(tile):
         return tile.rearrange("(f a) c -> a f c", a=PAIR)
 
+    x_by_head = x.rearrange("(b a f) c -> a f b c", a=PAIR, f=HEAD)
+
     def head_rows(block, a):
         return slice((block * PAIR + a) * HEAD, (block * PAIR + a + 1) * HEAD)
 
@@ -41,23 +43,24 @@ def tile_model_lite_kernel(tc, x, rope, offs, out):
         for a in range(PAIR):
             nc.sync.dma_start(by_head(cosines[:])[a], rope[0:HEAD, :])
 
-        rows_of = [work.tile([PARTITIONS, columns], F32, name="rows") for block in range(blocks)]
+        rows = held.tile([PARTITIONS, blocks, columns], F32, name="rows")
 
-        def load_rows(block, begin, end):
+        def load_rows(first, beyond):
             for a in range(PAIR):
-                nc.sync.dma_start(by_head(rows_of[block][:, begin:end])[a], x[head_rows(block, a), begin:end])
+                nc.sync.dma_start(
+                    rows[:, first:beyond, :].rearrange("(f a) b c -> a f b c", a=PAIR)[a],
+                    x_by_head[a, :, first:beyond, :],
+                )
 
-        parts_of = [[(0, LEAD), (LEAD, columns)]] + [[(0, columns)] for block in range(1, last)]
-        for block in range(last):
-            for begin, end in parts_of[block]:
-                load_rows(block, begin, end)
+        load_rows(0, 1)
+        load_rows(1, last)
 
         sines = held.tile([PARTITIONS, positions], F32, name="sines")
         for a in range(PAIR):
             nc.sync.dma_start(by_head(sines[:])[a, 0:HALF], rope[HEAD + HALF : 2 * HEAD, :])
             nc.sync.dma_start(by_head(sines[:])[a, HALF:HEAD], rope[HEAD : HEAD + HALF, :])
 
-        load_rows(last, 0, columns)
+        load_rows(last, blocks)
 
         keep = held.tile([PARTITIONS, PARTITIONS], F32, name="keep")
         make_identity(nc, keep[:])
@@ -66,6 +69,7 @@ def tile_model_lite_kernel(tc, x, rope, offs, out):
         nc.scalar.mul(turn[:, 0:middle], keep[:, middle:PARTITIONS], -1.0)
         nc.scalar.copy(turn[:, middle:PARTITIONS], keep[:, 0:middle])
 
+        parts_of = [[(0, LEAD), (LEAD, columns)]] + [[(0, columns)] for block in range(1, last)]
         total_of = [[sums.tile([PARTITIONS, end - begin], F32, name="total") for begin, end in parts] for parts in parts_of]
         for block in range(last):
             with_cosines = work.tile([PARTITIONS, columns], F32, name="with_cosines")
@@ -73,14 +77,14 @@ def tile_model_lite_kernel(tc, x, rope, offs, out):
                 nc.vector.tensor_tensor(
                     with_cosines[:, begin:end],
                     cosines[:].indirect(offsets[:, begin // 16 : end // 16]),
-                    rows_of[block][:, begin:end],
+                    rows[:, block, begin:end],
                     MULT,
                 )
                 nc.tensor.matmul(total[:], keep[:], with_cosines[:, begin:end], start=True, stop=False)
 
         for block in range(last):
             with_sines = work.tile([PARTITIONS, columns], F32, name="with_sines")
-            nc.vector.tensor_tensor(with_sines[:], sines[:].indirect(offsets[:]), rows_of[block][:], MULT)
+            nc.vector.tensor_tensor(with_sines[:], sines[:].indirect(offsets[:]), rows[:, block, :], MULT)
             rotated = work.tile([PARTITIONS, columns], F32, name="rotated")
             for (begin, end), total in zip(parts_of[block], total_of[block]):
                 nc.tensor.matmul(total[:], turn[:], with_sines[:, begin:end], start=False, stop=True)
@@ -91,12 +95,12 @@ def tile_model_lite_kernel(tc, x, rope, offs, out):
         width = columns // PIECES
         pieces = [slice(piece * width, (piece + 1) * width) for piece in range(PIECES)]
         with_sines = work.tile([PARTITIONS, columns], F32, name="with_sines")
-        nc.vector.tensor_tensor(with_sines[:], sines[:].indirect(offsets[:]), rows_of[last][:], MULT)
+        nc.vector.tensor_tensor(with_sines[:], sines[:].indirect(offsets[:]), rows[:, last, :], MULT)
         turned_of = [sums.tile([PARTITIONS, width], F32, name="total") for cols in pieces]
         for cols, turned in zip(pieces, turned_of):
             nc.tensor.matmul(turned[:], turn[:], with_sines[:, cols], start=True, stop=True)
         with_cosines = work.tile([PARTITIONS, columns], F32, name="with_cosines")
-        nc.vector.tensor_tensor(with_cosines[:], cosines[:].indirect(offsets[:]), rows_of[last][:], MULT)
+        nc.vector.tensor_tensor(with_cosines[:], cosines[:].indirect(offsets[:]), rows[:, last, :], MULT)
         rotated = work.tile([PARTITIONS, columns], F32, name="rotated")
         for cols, turned in zip(pieces, turned_of):
             nc.vector.tensor_tensor(rotated[:, cols], with_cosines[:, cols], turned[:], ADD)

@@ -13,6 +13,8 @@ PAIR = PARTITIONS // HEAD
 PIECES = 2
 LEAD = 128
 
+SPREAD = {2: "(i s) c -> s i c", 3: "(i s) b c -> s i b c"}
+
 FLOPS = 3 * 512 * 512
 
 
@@ -23,10 +25,13 @@ def tile_model_lite_kernel(tc, x, rope, offs, out):
     blocks = channels // PARTITIONS
     last = blocks - 1
 
-    def by_head(tile):
-        return tile.rearrange("(f a) c -> a f c", a=PAIR)
+    def every_second(view, start):
+        return view.rearrange(SPREAD[len(view.shape)], s=2)[start]
 
-    x_by_head = x.rearrange("(b a f) c -> a f b c", a=PAIR, f=HEAD)
+    def every_fourth(view, start):
+        return view.rearrange(SPREAD[len(view.shape)], s=4)[start]
+
+    x_by_block = x.rearrange("(b r) c -> r b c", r=PARTITIONS)
 
     def head_rows(block, a):
         return slice((block * PAIR + a) * HEAD, (block * PAIR + a + 1) * HEAD)
@@ -41,33 +46,49 @@ def tile_model_lite_kernel(tc, x, rope, offs, out):
 
         cosines = held.tile([PARTITIONS, positions], F32, name="cosines")
         for a in range(PAIR):
-            nc.sync.dma_start(by_head(cosines[:])[a], rope[0:HEAD, :])
+            nc.sync.dma_start(every_second(cosines[:], a), rope[0:HEAD, :])
 
         rows = held.tile([PARTITIONS, blocks, columns], F32, name="rows")
 
-        def load_rows(first, beyond):
+        def load_rows(first, beyond, begin, end):
             for a in range(PAIR):
                 nc.sync.dma_start(
-                    rows[:, first:beyond, :].rearrange("(f a) b c -> a f b c", a=PAIR)[a],
-                    x_by_head[a, :, first:beyond, :],
+                    every_second(rows[:, first:beyond, begin:end], a),
+                    x_by_block[a * HEAD : (a + 1) * HEAD, first:beyond, begin:end],
                 )
 
-        load_rows(0, 1)
-        load_rows(1, last)
+        load_rows(0, 1, 0, LEAD)
+        load_rows(0, 1, LEAD, columns)
+        load_rows(1, last, 0, columns)
 
         sines = held.tile([PARTITIONS, positions], F32, name="sines")
-        for a in range(PAIR):
-            nc.sync.dma_start(by_head(sines[:])[a, 0:HALF], rope[HEAD + HALF : 2 * HEAD, :])
-            nc.sync.dma_start(by_head(sines[:])[a, HALF:HEAD], rope[HEAD : HEAD + HALF, :])
+        nc.sync.dma_start(every_second(sines[:], 0), rope[HEAD : 2 * HEAD, :])
+        nc.sync.dma_start(every_fourth(sines[:], 1), rope[HEAD : HEAD + HALF, :])
+        nc.sync.dma_start(every_fourth(sines[:], 3), rope[HEAD + HALF : 2 * HEAD, :])
 
-        load_rows(last, blocks)
+        partners = held.tile([PARTITIONS, blocks, columns], F32, name="partners")
+
+        def load_partners(first, beyond):
+            tile = partners[:, first:beyond, :]
+            nc.sync.dma_start(every_second(tile, 0), x_by_block[HALF : HALF + HEAD, first:beyond, :])
+            nc.sync.dma_start(every_fourth(tile, 1), x_by_block[HEAD + HALF : PARTITIONS, first:beyond, :])
+            nc.sync.dma_start(every_fourth(tile, 3), x_by_block[0:HALF, first:beyond, :])
+
+        load_partners(0, 1)
+        load_partners(1, 2)
+        load_partners(2, blocks)
+        load_rows(last, blocks, 0, columns)
 
         keep = held.tile([PARTITIONS, PARTITIONS], F32, name="keep")
         make_identity(nc, keep[:])
         turn = held.tile([PARTITIONS, PARTITIONS], F32, name="turn")
-        middle = PARTITIONS // 2
-        nc.scalar.mul(turn[:, 0:middle], keep[:, middle:PARTITIONS], -1.0)
-        nc.scalar.copy(turn[:, middle:PARTITIONS], keep[:, 0:middle])
+        turn_of = turn[:].rearrange("k (f a) -> k a f", a=PAIR)
+        keep_second = keep[:].rearrange("k (i s) -> k s i", s=2)
+        keep_fourth = keep[:].rearrange("k (i s) -> k s i", s=4)
+        nc.scalar.mul(turn_of[:, 0, 0:HALF], keep_second[:, 0, 0:HALF], -1.0)
+        nc.scalar.copy(turn_of[:, 0, HALF:HEAD], keep_fourth[:, 3, :])
+        nc.scalar.mul(turn_of[:, 1, 0:HALF], keep_fourth[:, 1, :], -1.0)
+        nc.scalar.copy(turn_of[:, 1, HALF:HEAD], keep_second[:, 0, HALF:HEAD])
 
         parts_of = [[(0, LEAD), (LEAD, columns)]] + [[(0, columns)] for block in range(1, last)]
         total_of = [[sums.tile([PARTITIONS, end - begin], F32, name="total") for begin, end in parts] for parts in parts_of]
@@ -84,18 +105,18 @@ def tile_model_lite_kernel(tc, x, rope, offs, out):
 
         for block in range(last):
             with_sines = work.tile([PARTITIONS, columns], F32, name="with_sines")
-            nc.vector.tensor_tensor(with_sines[:], sines[:].indirect(offsets[:]), rows[:, block, :], MULT)
+            nc.vector.tensor_tensor(with_sines[:], sines[:].indirect(offsets[:]), partners[:, block, :], MULT)
             rotated = work.tile([PARTITIONS, columns], F32, name="rotated")
             for (begin, end), total in zip(parts_of[block], total_of[block]):
                 nc.tensor.matmul(total[:], turn[:], with_sines[:, begin:end], start=False, stop=True)
                 nc.scalar.copy(rotated[:, begin:end], total[:])
             for a in range(PAIR):
-                nc.sync.dma_start(out[head_rows(block, a), :], by_head(rotated[:])[a])
+                nc.sync.dma_start(out[head_rows(block, a), :], every_second(rotated[:], a))
 
         width = columns // PIECES
         pieces = [slice(piece * width, (piece + 1) * width) for piece in range(PIECES)]
         with_sines = work.tile([PARTITIONS, columns], F32, name="with_sines")
-        nc.vector.tensor_tensor(with_sines[:], sines[:].indirect(offsets[:]), rows[:, last, :], MULT)
+        nc.vector.tensor_tensor(with_sines[:], sines[:].indirect(offsets[:]), partners[:, last, :], MULT)
         turned_of = [sums.tile([PARTITIONS, width], F32, name="total") for cols in pieces]
         for cols, turned in zip(pieces, turned_of):
             nc.tensor.matmul(turned[:], turn[:], with_sines[:, cols], start=True, stop=True)
@@ -105,4 +126,4 @@ def tile_model_lite_kernel(tc, x, rope, offs, out):
         for cols, turned in zip(pieces, turned_of):
             nc.vector.tensor_tensor(rotated[:, cols], with_cosines[:, cols], turned[:], ADD)
             for a in range(PAIR):
-                nc.sync.dma_start(out[head_rows(last, a), cols], by_head(rotated[:, cols])[a])
+                nc.sync.dma_start(out[head_rows(last, a), cols], every_second(rotated[:, cols], a))

@@ -59,7 +59,8 @@ def tile_model_lite_kernel(tc, x, rope, offs, out):
 
         load_rows(0, 1, 0, LEAD)
         load_rows(0, 1, LEAD, columns)
-        load_rows(1, last, 0, columns)
+        for block in range(1, last):
+            load_rows(block, block + 1, 0, columns)
 
         sines = held.tile([PARTITIONS, positions], F32, name="sines")
         nc.sync.dma_start(every_second(sines[:], 0), rope[HEAD : 2 * HEAD, :])

import concourse.mybir as mybir
from concourse.masks import make_identity

F32 = mybir.dt.float32
U16 = mybir.dt.uint16
MULT = mybir.AluOpType.mult
ADD = mybir.AluOpType.add

PARTITIONS = 128
HEAD = 64
HALF = 32
PAIR = PARTITIONS // HEAD
PIECES = 2
LEAD = 128

SPREAD = {2: "(i s) c -> s i c", 3: "(i s) b c -> s i b c"}

FLOPS = 3 * 512 * 512


def tile_model_lite_kernel(tc, x, rope, offs, out):
    nc = tc.nc
    channels, columns = x.shape
    positions = rope.shape[1]
    blocks = channels // PARTITIONS
    last = blocks - 1

    def every_second(view, start):
        return view.rearrange(SPREAD[len(view.shape)], s=2)[start]

    def every_fourth(view, start):
        return view.rearrange(SPREAD[len(view.shape)], s=4)[start]

    x_by_block = x.rearrange("(b r) c -> r b c", r=PARTITIONS)

    def head_rows(block, a):
        return slice((block * PAIR + a) * HEAD, (block * PAIR + a + 1) * HEAD)

    with (
        tc.tile_pool(name="held", bufs=1) as held,
        tc.tile_pool(name="work", bufs=blocks) as work,
        tc.psum_pool(name="sums", bufs=last + 1 + PIECES) as sums,
    ):
        offsets = held.tile([PARTITIONS, columns // 16], U16, name="offsets")
        nc.sync.dma_start(offsets[:], offs)

        cosines = held.tile([PARTITIONS, positions], F32, name="cosines")
        for a in range(PAIR):
            nc.sync.dma_start(every_second(cosines[:], a), rope[0:HEAD, :])

        rows = held.tile([PARTITIONS, blocks, columns], F32, name="rows")

        def load_rows(first, beyond, begin, end):
            for a in range(PAIR):
                nc.sync.dma_start(
                    every_second(rows[:, first:beyond, begin:end], a),
                    x_by_block[a * HEAD : (a + 1) * HEAD, first:beyond, begin:end],
                )

        load_rows(0, 1, 0, LEAD)
        load_rows(0, 1, LEAD, columns)
        for block in range(1, last):
            load_rows(block, block + 1, 0, columns)

        sines = held.tile([PARTITIONS, positions], F32, name="sines")
        nc.sync.dma_start(every_second(sines[:], 0), rope[HEAD : 2 * HEAD, :])
        nc.sync.dma_start(every_fourth(sines[:], 1), rope[HEAD : HEAD + HALF, :])
        nc.sync.dma_start(every_fourth(sines[:], 3), rope[HEAD + HALF : 2 * HEAD, :])

        partners = held.tile([PARTITIONS, blocks, columns], F32, name="partners")

        def load_partners(first, beyond):
            tile = partners[:, first:beyond, :]
            nc.sync.dma_start(every_second(tile, 0), x_by_block[HALF : HALF + HEAD, first:beyond, :])
            nc.sync.dma_start(every_fourth(tile, 1), x_by_block[HEAD + HALF : PARTITIONS, first:beyond, :])
            nc.sync.dma_start(every_fourth(tile, 3), x_by_block[0:HALF, first:beyond, :])

        load_partners(0, 1)
        load_partners(1, 2)
        load_partners(2, blocks)
        load_rows(last, blocks, 0, columns)

        keep = held.tile([PARTITIONS, PARTITIONS], F32, name="keep")
        make_identity(nc, keep[:])
        turn = held.tile([PARTITIONS, PARTITIONS], F32, name="turn")
        turn_of = turn[:].rearrange("k (f a) -> k a f", a=PAIR)
        keep_second = keep[:].rearrange("k (i s) -> k s i", s=2)
        keep_fourth = keep[:].rearrange("k (i s) -> k s i", s=4)
        nc.scalar.mul(turn_of[:, 0, 0:HALF], keep_second[:, 0, 0:HALF], -1.0)
        nc.scalar.copy(turn_of[:, 0, HALF:HEAD], keep_fourth[:, 3, :])
        nc.scalar.mul(turn_of[:, 1, 0:HALF], keep_fourth[:, 1, :], -1.0)
        nc.scalar.copy(turn_of[:, 1, HALF:HEAD], keep_second[:, 0, HALF:HEAD])

        parts_of = [[(0, LEAD), (LEAD, columns)]] + [[(0, columns)] for block in range(1, last)]
        total_of = [[sums.tile([PARTITIONS, end - begin], F32, name="total") for begin, end in parts] for parts in parts_of]
        for block in range(last):
            with_cosines = work.tile([PARTITIONS, columns], F32, name="with_cosines")
            for (begin, end), total in zip(parts_of[block], total_of[block]):
                nc.vector.tensor_tensor(
                    with_cosines[:, begin:end],
                    cosines[:].indirect(offsets[:, begin // 16 : end // 16]),
                    rows[:, block, begin:end],
                    MULT,
                )
                nc.tensor.matmul(total[:], keep[:], with_cosines[:, begin:end], start=True, stop=False)

        for block in range(last):
            with_sines = work.tile([PARTITIONS, columns], F32, name="with_sines")
            nc.vector.tensor_tensor(with_sines[:], sines[:].indirect(offsets[:]), partners[:, block, :], MULT)
            rotated = work.tile([PARTITIONS, columns], F32, name="rotated")
            for (begin, end), total in zip(parts_of[block], total_of[block]):
                nc.tensor.matmul(total[:], turn[:], with_sines[:, begin:end], start=False, stop=True)
                nc.scalar.copy(rotated[:, begin:end], total[:])
            for a in range(PAIR):
                nc.sync.dma_start(out[head_rows(block, a), :], every_second(rotated[:], a))

        width = columns // PIECES
        pieces = [slice(piece * width, (piece + 1) * width) for piece in range(PIECES)]
        with_sines = work.tile([PARTITIONS, columns], F32, name="with_sines")
        nc.vector.tensor_tensor(with_sines[:], sines[:].indirect(offsets[:]), partners[:, last, :], MULT)
        turned_of = [sums.tile([PARTITIONS, width], F32, name="total") for cols in pieces]
        for cols, turned in zip(pieces, turned_of):
            nc.tensor.matmul(turned[:], turn[:], with_sines[:, cols], start=True, stop=True)
        with_cosines = work.tile([PARTITIONS, columns], F32, name="with_cosines")
        nc.vector.tensor_tensor(with_cosines[:], cosines[:].indirect(offsets[:]), rows[:, last, :], MULT)
        rotated = work.tile([PARTITIONS, columns], F32, name="rotated")
        for cols, turned in zip(pieces, turned_of):
            nc.vector.tensor_tensor(rotated[:, cols], with_cosines[:, cols], turned[:], ADD)
            for a in range(PAIR):
                nc.sync.dma_start(out[head_rows(last, a), cols], every_second(rotated[:, cols], a))
